import numpy as np
import ml_dtypes


def mxq(x, axis, fmt="e4m3"):
    dtype, down = {"e4m3": (ml_dtypes.float8_e4m3fn, 7), "e5m2": (ml_dtypes.float8_e5m2, 14)}[fmt]
    v = np.moveaxis(np.asarray(x, np.float32).astype(ml_dtypes.bfloat16).astype(np.float64), axis, -1)
    blocks = v.reshape(v.shape[:-1] + (-1, 32))
    amax = np.abs(blocks).max(-1, keepdims=True)
    byte = np.maximum(np.where(amax > 0, np.frexp(amax)[1] - 1 + 127, 0) - down, 1)
    scale = np.exp2(byte - 127.0)
    codes = (blocks / scale).astype(np.float32).astype(dtype).astype(np.float64)
    return np.moveaxis((codes * scale).reshape(v.shape), -1, axis)


WIDE = False


def mx_kscale(k):
    if not WIDE:
        return np.ones(k)
    levels = np.array([10, -10, 5, -5, 0])
    a = np.random.permutation(np.resize(levels, k // 512 * 4)).reshape(k // 512, 4)
    idx = np.arange(k)
    return np.exp2(a[idx // 512, idx % 128 // 32])


BF16 = ml_dtypes.bfloat16


def bf(x):
    return np.asarray(x, np.float32).astype(BF16)


def f64(x):
    return np.asarray(x).astype(np.float64)


B, C, N, T, KC = 16, 32, 512, 12, 3
EDGE_PROB = 0.01
ISO_PROB = 0.02


def setup_inputs():
    s = mx_kscale(N)
    u = np.random.random((N, N))
    adj = (u < EDGE_PROB).astype(np.float64)
    adj = np.maximum(adj, adj.T)
    keep = (np.random.random(N) >= ISO_PROB).astype(np.float64)
    adj = adj * keep[:, None] * keep[None, :]
    adj = adj * (s * s)[:, None]
    return {"x": bf(np.random.standard_normal((B, C, N, T)) * s[None, None, :, None]), "adj": bf(adj)}


def reference(x, adj):
    x, adj = f64(x), f64(adj)
    h = x.transpose(0, 3, 2, 1)
    d = adj.sum(-1)
    d_inv_sqrt = np.where(d > 0, np.where(d > 0, d, 1.0) ** -0.5, 0.0)
    norm_adj = d_inv_sqrt[:, None] * adj * d_inv_sqrt[None, :]
    lap = np.eye(N) - norm_adj
    lq = mxq(lap, 1, "e4m3")
    tx1 = lq @ mxq(h, 2, "e4m3")
    tx2 = 2.0 * (lq @ mxq(tx1, 2, "e4m3")) - h
    return tx1, tx2

@@ -1,0 +1,183 @@
+from contextlib import ExitStack
+
+import concourse.mybir as mybir
+from concourse.masks import make_identity
+
+F32 = mybir.dt.float32
+BF16 = mybir.dt.bfloat16
+U32 = mybir.dt.uint32
+U8 = mybir.dt.uint8
+FP8X4 = mybir.dt.float8_e4m3fn_x4
+ALU = mybir.AluOpType
+ACT = mybir.ActivationFunctionType
+AXIS = mybir.AxisListType
+
+P = 128
+PACK = 4
+B, C, N, T = 16, 32, 512, 12
+BPG = P // C
+GROUPS = B // BPG
+UNITS = 4
+CHUNK = UNITS * P
+
+FLOPS = 2 * 2 * N * N * B * T * C
+
+
+def tile_adaptivegraphconv_pa_t_kernel(tc, x, adj, out_0, out_1):
+    nc = tc.nc
+    with ExitStack() as ctx:
+        const = ctx.enter_context(tc.tile_pool(name="const", bufs=1))
+        xin = ctx.enter_context(tc.tile_pool(name="xin", bufs=GROUPS))
+        keep = ctx.enter_context(tc.tile_pool(name="keep", bufs=1))
+        work = ctx.enter_context(tc.tile_pool(name="work", bufs=2))
+        stage = ctx.enter_context(tc.tile_pool(name="stage", bufs=3))
+        psum_t = ctx.enter_context(tc.psum_pool(name="psum_t", bufs=2))
+        psum_1 = ctx.enter_context(tc.psum_pool(name="psum_1", bufs=2))
+        psum_2 = ctx.enter_context(tc.psum_pool(name="psum_2", bufs=4))
+
+        adj_rows = const.tile([P, PACK, N], BF16)
+        nc.sync.dma_start(out=adj_rows[:], in_=adj.rearrange("(p j) k -> p j k", j=PACK))
+        x_rows = x.rearrange("b c n t -> (b c) (n t)")
+        x_tiles = []
+        for g in range(GROUPS):
+            x_sb = xin.tile([P, N * T], BF16, name="x_sb")
+            nc.sync.dma_start(out=x_sb[:], in_=x_rows[g * P : (g + 1) * P, :])
+            x_tiles.append(x_sb)
+
+        ident = const.tile([P, P], F32)
+        make_identity(nc, ident[:])
+        eye = const.tile([P, PACK, P, PACK], BF16)
+        nc.vector.memset(eye[:], 0.0)
+        for j in range(PACK):
+            nc.vector.tensor_copy(out=eye[:, j, :, j], in_=ident[:])
+        one = const.tile([P, 1], F32)
+        nc.vector.memset(one[:], 1.0)
+        warm = const.tile([P, 1], F32)
+        nc.scalar.activation(out=warm[:], in_=one[:], func=ACT.Sqrt)
+
+        d = const.tile([P, PACK], F32)
+        nc.vector.tensor_reduce(out=d[:], in_=adj_rows[:], axis=AXIS.X, op=ALU.add)
+        d_safe = const.tile([P, PACK], F32)
+        nc.vector.scalar_tensor_tensor(
+            out=d_safe[:], in0=d[:], scalar=0.0, in1=d[:], op0=ALU.is_le, op1=ALU.add
+        )
+        root = const.tile([P, PACK], F32)
+        nc.scalar.activation(out=root[:], in_=d_safe[:], func=ACT.Sqrt)
+        r_all = const.tile([P, PACK], F32)
+        nc.vector.reciprocal(out=r_all[:], in_=root[:])
+        r = const.tile([P, PACK], F32)
+        nc.vector.scalar_tensor_tensor(
+            out=r[:], in0=d[:], scalar=0.0, in1=r_all[:], op0=ALU.is_gt, op1=ALU.mult
+        )
+        r_neg = const.tile([P, PACK], F32)
+        nc.vector.tensor_scalar(out=r_neg[:], in0=r[:], scalar1=-1.0, scalar2=None, op0=ALU.mult)
+
+        rows_scaled = const.tile([P, PACK, PACK, P], F32)
+        for j in range(PACK):
+            adj_by_t = adj_rows[:, j, :].rearrange("p (k t) -> p t k", t=PACK)
+            if j % 2 == 0:
+                nc.vector.tensor_scalar(
+                    out=rows_scaled[:, j], in0=adj_by_t, scalar1=r_neg[:, j : j + 1],
+                    scalar2=None, op0=ALU.mult,
+                )
+            else:
+                nc.scalar.activation(
+                    out=rows_scaled[:, j], in_=adj_by_t, func=ACT.Copy, scale=r_neg[:, j : j + 1]
+                )
+        l_grouped = const.tile([P, PACK, P, PACK], BF16, align_bytes=64)
+        for j in range(PACK):
+            lt = psum_t.tile([P, PACK, P], F32, tag="tr")
+            for t in range(PACK):
+                nc.tensor.transpose(lt[:, t, :], rows_scaled[:, j, t, :], ident[:])
+            neg_norm = work.tile([P, P, PACK], F32)
+            nc.vector.tensor_tensor(
+                out=neg_norm[:], in0=lt[:].rearrange("k t p -> k p t"),
+                in1=r[:].unsqueeze(1).to_broadcast([P, P, PACK]), op=ALU.mult,
+            )
+            nc.vector.tensor_tensor(
+                out=l_grouped[:, j], in0=neg_norm[:], in1=eye[:, j], op=ALU.add
+            )
+        l_codes = const.tile([P, PACK * P], U32, align_bytes=64)
+        l_scales = const.tile([P, PACK * P], U8, align_bytes=64)
+        nc.vector.quantize_mx(
+            out=l_codes[:].bitcast(FP8X4), scales=l_scales[:],
+            in_=l_grouped[:].rearrange("k j p t -> k (j p t)"),
+        )
+
+        def l_rows(j):
+            cols = slice(j * P, (j + 1) * P)
+            return {"lhsT": l_codes[:, cols].bitcast(FP8X4), "lhsT_scale": l_scales[:, cols]}
+
+        h_grouped = keep.tile([P, GROUPS, T, P, PACK], BF16, align_bytes=64)
+        h_codes = keep.tile([P, GROUPS, T, P], U32, align_bytes=64)
+        h_scales = keep.tile([P, GROUPS, T, P], U8, align_bytes=64)
+
+        for g in range(GROUPS):
+            batches = slice(g * BPG, (g + 1) * BPG)
+            x_words = x_tiles[g][:].bitcast(F32).rearrange(
+                "r (p j u) -> r p j u", j=PACK, u=T // 2
+            )
+            for t0 in range(0, T, UNITS):
+                steps = slice(t0, t0 + UNITS)
+                for u in range(t0 // 2, (t0 + UNITS) // 2):
+                    xt = psum_t.tile([P, PACK, P], F32, tag="tr")
+                    for j in range(PACK):
+                        nc.tensor.transpose(xt[:, j, :], x_words[:, :, j, u], ident[:])
+                    nc.scalar.copy(
+                        out=h_grouped[:, g, 2 * u : 2 * u + 2],
+                        in_=xt[:].rearrange("p j w -> p (j w)").bitcast(BF16).rearrange(
+                            "p (j w e) -> p e w j", j=PACK, e=2
+                        ),
+                    )
+                nc.vector.quantize_mx(
+                    out=h_codes[:, g, steps].rearrange("p i w -> p (i w)").bitcast(FP8X4),
+                    scales=h_scales[:, g, steps].rearrange("p i w -> p (i w)"),
+                    in_=h_grouped[:, g, steps].rearrange("p i w j -> p (i w j)"),
+                )
+
+                tx1_stage = stage.tile([P, UNITS, BPG, PACK, C], F32)
+                for i in range(UNITS):
+                    s1 = psum_1.tile([P, PACK, P], F32)
+                    for j in range(PACK):
+                        nc.tensor.matmul_mx(
+                            out=s1[:, j, :],
+                            rhs=h_codes[:, g, t0 + i, :].bitcast(FP8X4),
+                            rhs_scale=h_scales[:, g, t0 + i, :],
+                            start=True, stop=True, **l_rows(j),
+                        )
+                    nc.scalar.copy(
+                        out=tx1_stage[:, i], in_=s1[:].rearrange("p j (b c) -> p b j c", c=C)
+                    )
+                    nc.sync.dma_start(
+                        out=out_0[batches, t0 + i].rearrange("b (p j) c -> p b (j c)", j=PACK),
+                        in_=tx1_stage[:, i].rearrange("p b j c -> p b (j c)"),
+                    )
+                tx1_grouped = work.tile([P, UNITS * BPG, C, PACK], BF16, align_bytes=64)
+                nc.vector.tensor_copy(
+                    out=tx1_grouped[:], in_=tx1_stage[:].rearrange("p i b j c -> p (i b) c j")
+                )
+                t_codes = work.tile([P, CHUNK], U32, align_bytes=64)
+                t_scales = work.tile([P, CHUNK], U8, align_bytes=64)
+                nc.vector.quantize_mx(
+                    out=t_codes[:].bitcast(FP8X4), scales=t_scales[:],
+                    in_=tx1_grouped[:].rearrange("p q c j -> p (q c j)"),
+                )
+
+                tx2_stage = stage.tile([P, UNITS * BPG, PACK, C], F32)
+                h_chunk = h_grouped[:, g, steps].rearrange("p i (b c) j -> p (i b) c j", c=C)
+                for j in range(PACK):
+                    s2 = psum_2.tile([P, CHUNK], F32)
+                    nc.tensor.matmul_mx(
+                        out=s2[:], rhs=t_codes[:].bitcast(FP8X4), rhs_scale=t_scales[:],
+                        start=True, stop=True, **l_rows(j),
+                    )
+                    nc.vector.scalar_tensor_tensor(
+                        out=tx2_stage[:, :, j, :],
+                        in0=s2[:].rearrange("p (q c) -> p q c", c=C), scalar=2.0,
+                        in1=h_chunk[:, :, :, j], op0=ALU.mult, op1=ALU.subtract,
+                    )
+                for i in range(UNITS):
+                    nc.sync.dma_start(
+                        out=out_1[batches, t0 + i].rearrange("b (p j) c -> p b (j c)", j=PACK),
+                        in_=tx2_stage[:, i * BPG : (i + 1) * BPG].rearrange("p b j c -> p b (j c)"),
+                    )

@@ -17,8 +17,11 @@ PACK = 4
 B, C, N, T = 16, 32, 512, 12
 BPG = P // C
 GROUPS = B // BPG
-UNITS = 4
-CHUNK = UNITS * P
+STEPS = P // C
+QUADS = T // STEPS
+CHUNK = BPG * P
+SQ = 32
+RUN = N // SQ
 
 FLOPS = 2 * 2 * N * N * B * T * C
 
@@ -30,10 +33,12 @@ def tile_adaptivegraphconv_pa_t_kernel(tc, x, adj, out_0, out_1):
         xin = ctx.enter_context(tc.tile_pool(name="xin", bufs=GROUPS))
         keep = ctx.enter_context(tc.tile_pool(name="keep", bufs=1))
         work = ctx.enter_context(tc.tile_pool(name="work", bufs=2))
-        stage = ctx.enter_context(tc.tile_pool(name="stage", bufs=3))
+        stage1 = ctx.enter_context(tc.tile_pool(name="stage1", bufs=6))
+        stage2 = ctx.enter_context(tc.tile_pool(name="stage2", bufs=3))
         psum_t = ctx.enter_context(tc.psum_pool(name="psum_t", bufs=2))
-        psum_1 = ctx.enter_context(tc.psum_pool(name="psum_1", bufs=2))
-        psum_2 = ctx.enter_context(tc.psum_pool(name="psum_2", bufs=4))
+        psum_a = ctx.enter_context(tc.psum_pool(name="psum_a", bufs=2))
+        psum_y = ctx.enter_context(tc.psum_pool(name="psum_y", bufs=2))
+        psum_2 = ctx.enter_context(tc.psum_pool(name="psum_2", bufs=2))
 
         adj_rows = const.tile([P, PACK, N], BF16)
         nc.sync.dma_start(out=adj_rows[:], in_=adj.rearrange("(p j) k -> p j k", j=PACK))
@@ -85,6 +90,7 @@ def tile_adaptivegraphconv_pa_t_kernel(tc, x, adj, out_0, out_1):
                     out=rows_scaled[:, j], in_=adj_by_t, func=ACT.Copy, scale=r_neg[:, j : j + 1]
                 )
         l_grouped = const.tile([P, PACK, P, PACK], BF16, align_bytes=64)
+        l_spread = const.tile([P, RUN // PACK, PACK, SQ, PACK], BF16, align_bytes=64)
         for j in range(PACK):
             lt = psum_t.tile([P, PACK, P], F32, tag="tr")
             for t in range(PACK):
@@ -97,74 +103,93 @@ def tile_adaptivegraphconv_pa_t_kernel(tc, x, adj, out_0, out_1):
             nc.vector.tensor_tensor(
                 out=l_grouped[:, j], in0=neg_norm[:], in1=eye[:, j], op=ALU.add
             )
-        l_codes = const.tile([P, PACK * P], U32, align_bytes=64)
-        l_scales = const.tile([P, PACK * P], U8, align_bytes=64)
+            nc.scalar.copy(
+                out=l_spread[:, :, j],
+                in_=l_grouped[:, j].rearrange("k (q a) t -> k a q t", a=RUN // PACK),
+            )
+        l_codes = const.tile([P, N], U32, align_bytes=64)
+        l_scales = const.tile([P, N], U8, align_bytes=64)
         nc.vector.quantize_mx(
             out=l_codes[:].bitcast(FP8X4), scales=l_scales[:],
             in_=l_grouped[:].rearrange("k j p t -> k (j p t)"),
+        )
+        ls_codes = const.tile([P, N], U32, align_bytes=64)
+        ls_scales = const.tile([P, N], U8, align_bytes=64)
+        nc.vector.quantize_mx(
+            out=ls_codes[:].bitcast(FP8X4), scales=ls_scales[:],
+            in_=l_spread[:].rearrange("k a j q t -> k (a j q t)"),
         )
 
         def l_rows(j):
             cols = slice(j * P, (j + 1) * P)
             return {"lhsT": l_codes[:, cols].bitcast(FP8X4), "lhsT_scale": l_scales[:, cols]}
 
-        h_grouped = keep.tile([P, GROUPS, T, P, PACK], BF16, align_bytes=64)
-        h_codes = keep.tile([P, GROUPS, T, P], U32, align_bytes=64)
-        h_scales = keep.tile([P, GROUPS, T, P], U8, align_bytes=64)
+        h_grouped = keep.tile([P, GROUPS, QUADS, BPG, P, PACK], BF16, align_bytes=64)
+        h_codes = keep.tile([P, GROUPS, QUADS, BPG, P], U32, align_bytes=64)
+        h_scales = keep.tile([P, GROUPS, QUADS, BPG, P], U8, align_bytes=64)
 
         for g in range(GROUPS):
-            batches = slice(g * BPG, (g + 1) * BPG)
             x_words = x_tiles[g][:].bitcast(F32).rearrange(
                 "r (p j u) -> r p j u", j=PACK, u=T // 2
             )
-            for t0 in range(0, T, UNITS):
-                steps = slice(t0, t0 + UNITS)
-                for u in range(t0 // 2, (t0 + UNITS) // 2):
+            for s in range(QUADS):
+                steps = slice(s * STEPS, (s + 1) * STEPS)
+                for half in range(STEPS // 2):
                     xt = psum_t.tile([P, PACK, P], F32, tag="tr")
                     for j in range(PACK):
-                        nc.tensor.transpose(xt[:, j, :], x_words[:, :, j, u], ident[:])
-                    nc.scalar.copy(
-                        out=h_grouped[:, g, 2 * u : 2 * u + 2],
-                        in_=xt[:].rearrange("p j w -> p (j w)").bitcast(BF16).rearrange(
-                            "p (j w e) -> p e w j", j=PACK, e=2
-                        ),
+                        nc.tensor.transpose(
+                            xt[:, j, :], x_words[:, :, j, s * (STEPS // 2) + half], ident[:]
+                        )
+                    xt_steps = xt[:].rearrange("p j w -> p (j w)").bitcast(BF16).rearrange(
+                        "p (j b c e) -> p e b c j", j=PACK, b=BPG, e=2
                     )
+                    for e in range(2):
+                        i = 2 * half + e
+                        nc.scalar.copy(
+                            out=h_grouped[:, g, s, :, i * C : (i + 1) * C, :], in_=xt_steps[:, e]
+                        )
                 nc.vector.quantize_mx(
-                    out=h_codes[:, g, steps].rearrange("p i w -> p (i w)").bitcast(FP8X4),
-                    scales=h_scales[:, g, steps].rearrange("p i w -> p (i w)"),
-                    in_=h_grouped[:, g, steps].rearrange("p i w j -> p (i w j)"),
+                    out=h_codes[:, g, s].rearrange("p b w -> p (b w)").bitcast(FP8X4),
+                    scales=h_scales[:, g, s].rearrange("p b w -> p (b w)"),
+                    in_=h_grouped[:, g, s].rearrange("p b w j -> p (b w j)"),
                 )
 
-                tx1_stage = stage.tile([P, UNITS, BPG, PACK, C], F32)
-                for i in range(UNITS):
-                    s1 = psum_1.tile([P, PACK, P], F32)
+                tx1_grouped = work.tile([P, BPG, P, PACK], BF16, align_bytes=64)
+                for b in range(BPG):
+                    s1 = psum_a.tile([P, PACK, P], F32)
                     for j in range(PACK):
                         nc.tensor.matmul_mx(
                             out=s1[:, j, :],
-                            rhs=h_codes[:, g, t0 + i, :].bitcast(FP8X4),
-                            rhs_scale=h_scales[:, g, t0 + i, :],
+                            rhs=h_codes[:, g, s, b, :].bitcast(FP8X4),
+                            rhs_scale=h_scales[:, g, s, b, :],
                             start=True, stop=True, **l_rows(j),
                         )
-                    nc.scalar.copy(
-                        out=tx1_stage[:, i], in_=s1[:].rearrange("p j (b c) -> p b j c", c=C)
-                    )
-                    nc.sync.dma_start(
-                        out=out_0[batches, t0 + i].rearrange("b (p j) c -> p b (j c)", j=PACK),
-                        in_=tx1_stage[:, i].rearrange("p b j c -> p b (j c)"),
-                    )
-                tx1_grouped = work.tile([P, UNITS * BPG, C, PACK], BF16, align_bytes=64)
-                nc.vector.tensor_copy(
-                    out=tx1_grouped[:], in_=tx1_stage[:].rearrange("p i b j c -> p (i b) c j")
-                )
+                    nc.scalar.copy(out=tx1_grouped[:, b], in_=s1[:].rearrange("p j w -> p w j"))
                 t_codes = work.tile([P, CHUNK], U32, align_bytes=64)
                 t_scales = work.tile([P, CHUNK], U8, align_bytes=64)
                 nc.vector.quantize_mx(
                     out=t_codes[:].bitcast(FP8X4), scales=t_scales[:],
-                    in_=tx1_grouped[:].rearrange("p q c j -> p (q c j)"),
+                    in_=tx1_grouped[:].rearrange("p b w j -> p (b w j)"),
                 )
 
-                tx2_stage = stage.tile([P, UNITS * BPG, PACK, C], F32)
-                h_chunk = h_grouped[:, g, steps].rearrange("p i (b c) j -> p (i b) c j", c=C)
+                for b in range(BPG):
+                    y1 = psum_y.tile([P, N], F32)
+                    nc.tensor.matmul_mx(
+                        out=y1[:],
+                        lhsT=h_codes[:, g, s, b, :].bitcast(FP8X4),
+                        lhsT_scale=h_scales[:, g, s, b, :],
+                        rhs=ls_codes[:].bitcast(FP8X4), rhs_scale=ls_scales[:],
+                        start=True, stop=True,
+                    )
+                    z1 = stage1.tile([P, N], F32, align_bytes=64)
+                    nc.vector.transpose(out=z1[:], in_=y1[:])
+                    nc.sync.dma_start(
+                        out=out_0[g * BPG + b, steps].rearrange("i (q v) c -> (i q) (v c)", q=SQ),
+                        in_=z1[:],
+                    )
+
+                tx2_stage = stage2.tile([P, BPG * STEPS, PACK, C], F32)
+                h_chunk = h_grouped[:, g, s].rearrange("p b (i c) j -> p (b i) c j", c=C)
                 for j in range(PACK):
                     s2 = psum_2.tile([P, CHUNK], F32)
                     nc.tensor.matmul_mx(
@@ -176,8 +201,10 @@ def tile_adaptivegraphconv_pa_t_kernel(tc, x, adj, out_0, out_1):
                         in0=s2[:].rearrange("p (q c) -> p q c", c=C), scalar=2.0,
                         in1=h_chunk[:, :, :, j], op0=ALU.mult, op1=ALU.subtract,
                     )
-                for i in range(UNITS):
+                for b in range(BPG):
                     nc.sync.dma_start(
-                        out=out_1[batches, t0 + i].rearrange("b (p j) c -> p b (j c)", j=PACK),
-                        in_=tx2_stage[:, i * BPG : (i + 1) * BPG].rearrange("p b j c -> p b (j c)"),
+                        out=out_1[g * BPG + b, steps].rearrange("i (p j) c -> p i (j c)", j=PACK),
+                        in_=tx2_stage[:, b * STEPS : (b + 1) * STEPS].rearrange(
+                            "p i j c -> p i (j c)"
+                        ),
                     )

@@ -196,11 +196,18 @@ def tile_adaptivegraphconv_pa_t_kernel(tc, x, adj, out_0, out_1):
                         out=s2[:], rhs=t_codes[:].bitcast(FP8X4), rhs_scale=t_scales[:],
                         start=True, stop=True, **l_rows(j),
                     )
-                    nc.vector.scalar_tensor_tensor(
-                        out=tx2_stage[:, :, j, :],
-                        in0=s2[:].rearrange("p (q c) -> p q c", c=C), scalar=2.0,
-                        in1=h_chunk[:, :, :, j], op0=ALU.mult, op1=ALU.subtract,
-                    )
+                    sums = s2[:].rearrange("p (q c) -> p q c", c=C)
+                    if j < PACK - 1:
+                        nc.vector.scalar_tensor_tensor(
+                            out=tx2_stage[:, :, j, :], in0=sums, scalar=2.0,
+                            in1=h_chunk[:, :, :, j], op0=ALU.mult, op1=ALU.subtract,
+                        )
+                    else:
+                        nc.scalar.mul(out=tx2_stage[:, :, j, :], in_=sums, mul=2.0)
+                        nc.gpsimd.tensor_tensor(
+                            out=tx2_stage[:, :, j, :], in0=tx2_stage[:, :, j, :],
+                            in1=h_chunk[:, :, :, j], op=ALU.subtract,
+                        )
                 for b in range(BPG):
                     nc.sync.dma_start(
                         out=out_1[g * BPG + b, steps].rearrange("i (p j) c -> p i (j c)", j=PACK),

@@ -20,8 +20,10 @@ GROUPS = B // BPG
 STEPS = P // C
 QUADS = T // STEPS
 CHUNK = BPG * P
+CHUNKS = GROUPS * QUADS
 SQ = 32
 RUN = N // SQ
+AHEAD = 2
 
 FLOPS = 2 * 2 * N * N * B * T * C
 
@@ -29,16 +31,15 @@ FLOPS = 2 * 2 * N * N * B * T * C
 def tile_adaptivegraphconv_pa_t_kernel(tc, x, adj, out_0, out_1):
     nc = tc.nc
     with ExitStack() as ctx:
+        ctx.enter_context(tc.manual_schedule())
         const = ctx.enter_context(tc.tile_pool(name="const", bufs=1))
         xin = ctx.enter_context(tc.tile_pool(name="xin", bufs=GROUPS))
         keep = ctx.enter_context(tc.tile_pool(name="keep", bufs=1))
         work = ctx.enter_context(tc.tile_pool(name="work", bufs=2))
-        stage1 = ctx.enter_context(tc.tile_pool(name="stage1", bufs=6))
-        stage2 = ctx.enter_context(tc.tile_pool(name="stage2", bufs=3))
-        psum_t = ctx.enter_context(tc.psum_pool(name="psum_t", bufs=2))
-        psum_a = ctx.enter_context(tc.psum_pool(name="psum_a", bufs=2))
-        psum_y = ctx.enter_context(tc.psum_pool(name="psum_y", bufs=2))
-        psum_2 = ctx.enter_context(tc.psum_pool(name="psum_2", bufs=2))
+        stage1 = ctx.enter_context(tc.tile_pool(name="stage1", bufs=2 * BPG))
+        stage2 = ctx.enter_context(tc.tile_pool(name="stage2", bufs=4))
+        psum_tr = ctx.enter_context(tc.psum_pool(name="psum_tr", bufs=2))
+        psum_acc = ctx.enter_context(tc.psum_pool(name="psum_acc", bufs=6))
 
         adj_rows = const.tile([P, PACK, N], BF16)
         nc.sync.dma_start(out=adj_rows[:], in_=adj.rearrange("(p j) k -> p j k", j=PACK))
@@ -59,6 +60,38 @@ def tile_adaptivegraphconv_pa_t_kernel(tc, x, adj, out_0, out_1):
         nc.vector.memset(one[:], 1.0)
         warm = const.tile([P, 1], F32)
         nc.scalar.activation(out=warm[:], in_=one[:], func=ACT.Sqrt)
+
+        h_grouped = keep.tile([P, GROUPS, QUADS, BPG, P, PACK], BF16, align_bytes=64)
+        h_codes = keep.tile([P, GROUPS, QUADS, BPG, P], U32, align_bytes=64)
+        h_scales = keep.tile([P, GROUPS, QUADS, BPG, P], U8, align_bytes=64)
+
+        def transpose_x(k):
+            g, s = divmod(k, QUADS)
+            x_words = x_tiles[g][:].bitcast(F32).rearrange(
+                "r (p j u) -> r p j u", j=PACK, u=T // 2
+            )
+            for half in range(STEPS // 2):
+                xt = psum_tr.tile([P, PACK, P], F32)
+                for j in range(PACK):
+                    nc.tensor.transpose(
+                        xt[:, j, :], x_words[:, :, j, s * (STEPS // 2) + half], ident[:]
+                    )
+                xt_steps = xt[:].rearrange("p j w -> p (j w)").bitcast(BF16).rearrange(
+                    "p (j b c e) -> p e b c j", j=PACK, b=BPG, e=2
+                )
+                for e in range(2):
+                    i = 2 * half + e
+                    nc.scalar.copy(
+                        out=h_grouped[:, g, s, :, i * C : (i + 1) * C, :], in_=xt_steps[:, e]
+                    )
+
+        def quantise_h(k):
+            g, s = divmod(k, QUADS)
+            nc.vector.quantize_mx(
+                out=h_codes[:, g, s].rearrange("p b w -> p (b w)").bitcast(FP8X4),
+                scales=h_scales[:, g, s].rearrange("p b w -> p (b w)"),
+                in_=h_grouped[:, g, s].rearrange("p b w j -> p (b w j)"),
+            )
 
         d = const.tile([P, PACK], F32)
         nc.vector.tensor_reduce(out=d[:], in_=adj_rows[:], axis=AXIS.X, op=ALU.add)
@@ -89,10 +122,11 @@ def tile_adaptivegraphconv_pa_t_kernel(tc, x, adj, out_0, out_1):
                 nc.scalar.activation(
                     out=rows_scaled[:, j], in_=adj_by_t, func=ACT.Copy, scale=r_neg[:, j : j + 1]
                 )
+        transpose_x(0)
         l_grouped = const.tile([P, PACK, P, PACK], BF16, align_bytes=64)
         l_spread = const.tile([P, RUN // PACK, PACK, SQ, PACK], BF16, align_bytes=64)
         for j in range(PACK):
-            lt = psum_t.tile([P, PACK, P], F32, tag="tr")
+            lt = psum_acc.tile([P, PACK, P], F32, tag="acc")
             for t in range(PACK):
                 nc.tensor.transpose(lt[:, t, :], rows_scaled[:, j, t, :], ident[:])
             neg_norm = work.tile([P, P, PACK], F32)
@@ -113,105 +147,94 @@ def tile_adaptivegraphconv_pa_t_kernel(tc, x, adj, out_0, out_1):
             out=l_codes[:].bitcast(FP8X4), scales=l_scales[:],
             in_=l_grouped[:].rearrange("k j p t -> k (j p t)"),
         )
+        quantise_h(0)
         ls_codes = const.tile([P, N], U32, align_bytes=64)
         ls_scales = const.tile([P, N], U8, align_bytes=64)
         nc.vector.quantize_mx(
             out=ls_codes[:].bitcast(FP8X4), scales=ls_scales[:],
             in_=l_spread[:].rearrange("k a j q t -> k (a j q t)"),
         )
+        for k in range(1, AHEAD):
+            transpose_x(k)
 
         def l_rows(j):
             cols = slice(j * P, (j + 1) * P)
             return {"lhsT": l_codes[:, cols].bitcast(FP8X4), "lhsT_scale": l_scales[:, cols]}
 
-        h_grouped = keep.tile([P, GROUPS, QUADS, BPG, P, PACK], BF16, align_bytes=64)
-        h_codes = keep.tile([P, GROUPS, QUADS, BPG, P], U32, align_bytes=64)
-        h_scales = keep.tile([P, GROUPS, QUADS, BPG, P], U8, align_bytes=64)
-
-        for g in range(GROUPS):
-            x_words = x_tiles[g][:].bitcast(F32).rearrange(
-                "r (p j u) -> r p j u", j=PACK, u=T // 2
-            )
-            for s in range(QUADS):
-                steps = slice(s * STEPS, (s + 1) * STEPS)
-                for half in range(STEPS // 2):
-                    xt = psum_t.tile([P, PACK, P], F32, tag="tr")
-                    for j in range(PACK):
-                        nc.tensor.transpose(
-                            xt[:, j, :], x_words[:, :, j, s * (STEPS // 2) + half], ident[:]
-                        )
-                    xt_steps = xt[:].rearrange("p j w -> p (j w)").bitcast(BF16).rearrange(
-                        "p (j b c e) -> p e b c j", j=PACK, b=BPG, e=2
-                    )
-                    for e in range(2):
-                        i = 2 * half + e
-                        nc.scalar.copy(
-                            out=h_grouped[:, g, s, :, i * C : (i + 1) * C, :], in_=xt_steps[:, e]
-                        )
-                nc.vector.quantize_mx(
-                    out=h_codes[:, g, s].rearrange("p b w -> p (b w)").bitcast(FP8X4),
-                    scales=h_scales[:, g, s].rearrange("p b w -> p (b w)"),
-                    in_=h_grouped[:, g, s].rearrange("p b w j -> p (b w j)"),
-                )
-
-                tx1_grouped = work.tile([P, BPG, P, PACK], BF16, align_bytes=64)
-                for b in range(BPG):
-                    s1 = psum_a.tile([P, PACK, P], F32)
-                    for j in range(PACK):
-                        nc.tensor.matmul_mx(
-                            out=s1[:, j, :],
-                            rhs=h_codes[:, g, s, b, :].bitcast(FP8X4),
-                            rhs_scale=h_scales[:, g, s, b, :],
-                            start=True, stop=True, **l_rows(j),
-                        )
-                    nc.scalar.copy(out=tx1_grouped[:, b], in_=s1[:].rearrange("p j w -> p w j"))
-                t_codes = work.tile([P, CHUNK], U32, align_bytes=64)
-                t_scales = work.tile([P, CHUNK], U8, align_bytes=64)
-                nc.vector.quantize_mx(
-                    out=t_codes[:].bitcast(FP8X4), scales=t_scales[:],
-                    in_=tx1_grouped[:].rearrange("p b w j -> p (b w j)"),
-                )
-
-                for b in range(BPG):
-                    y1 = psum_y.tile([P, N], F32)
-                    nc.tensor.matmul_mx(
-                        out=y1[:],
-                        lhsT=h_codes[:, g, s, b, :].bitcast(FP8X4),
-                        lhsT_scale=h_scales[:, g, s, b, :],
-                        rhs=ls_codes[:].bitcast(FP8X4), rhs_scale=ls_scales[:],
-                        start=True, stop=True,
-                    )
-                    z1 = stage1.tile([P, N], F32, align_bytes=64)
-                    nc.vector.transpose(out=z1[:], in_=y1[:])
-                    nc.sync.dma_start(
-                        out=out_0[g * BPG + b, steps].rearrange("i (q v) c -> (i q) (v c)", q=SQ),
-                        in_=z1[:],
-                    )
-
-                tx2_stage = stage2.tile([P, BPG * STEPS, PACK, C], F32)
-                h_chunk = h_grouped[:, g, s].rearrange("p b (i c) j -> p (b i) c j", c=C)
+        def first_product(k):
+            g, s = divmod(k, QUADS)
+            tx1_grouped = work.tile([P, BPG, P, PACK], BF16, align_bytes=64)
+            for b in range(BPG):
+                unit = {
+                    "codes": h_codes[:, g, s, b, :].bitcast(FP8X4),
+                    "scales": h_scales[:, g, s, b, :],
+                }
+                s1 = psum_acc.tile([P, PACK, P], F32, tag="acc")
                 for j in range(PACK):
-                    s2 = psum_2.tile([P, CHUNK], F32)
                     nc.tensor.matmul_mx(
-                        out=s2[:], rhs=t_codes[:].bitcast(FP8X4), rhs_scale=t_scales[:],
+                        out=s1[:, j, :], rhs=unit["codes"], rhs_scale=unit["scales"],
                         start=True, stop=True, **l_rows(j),
                     )
-                    sums = s2[:].rearrange("p (q c) -> p q c", c=C)
-                    if j < PACK - 1:
-                        nc.vector.scalar_tensor_tensor(
-                            out=tx2_stage[:, :, j, :], in0=sums, scalar=2.0,
-                            in1=h_chunk[:, :, :, j], op0=ALU.mult, op1=ALU.subtract,
-                        )
-                    else:
-                        nc.scalar.mul(out=tx2_stage[:, :, j, :], in_=sums, mul=2.0)
-                        nc.gpsimd.tensor_tensor(
-                            out=tx2_stage[:, :, j, :], in0=tx2_stage[:, :, j, :],
-                            in1=h_chunk[:, :, :, j], op=ALU.subtract,
-                        )
-                for b in range(BPG):
-                    nc.sync.dma_start(
-                        out=out_1[g * BPG + b, steps].rearrange("i (p j) c -> p i (j c)", j=PACK),
-                        in_=tx2_stage[:, b * STEPS : (b + 1) * STEPS].rearrange(
-                            "p i j c -> p i (j c)"
-                        ),
+                nc.scalar.copy(out=tx1_grouped[:, b], in_=s1[:].rearrange("p j w -> p w j"))
+                y1 = psum_acc.tile([P, N], F32, tag="acc")
+                nc.tensor.matmul_mx(
+                    out=y1[:], lhsT=unit["codes"], lhsT_scale=unit["scales"],
+                    rhs=ls_codes[:].bitcast(FP8X4), rhs_scale=ls_scales[:],
+                    start=True, stop=True,
+                )
+                z1 = stage1.tile([P, N], F32, align_bytes=64)
+                nc.vector.transpose(out=z1[:], in_=y1[:])
+                nc.sync.dma_start(
+                    out=out_0[g * BPG + b, s * STEPS : (s + 1) * STEPS].rearrange(
+                        "i (q v) c -> (i q) (v c)", q=SQ
+                    ),
+                    in_=z1[:],
+                )
+            return tx1_grouped
+
+        def quantise_tx1(tx1_grouped):
+            t_codes = work.tile([P, CHUNK], U32, align_bytes=64)
+            t_scales = work.tile([P, CHUNK], U8, align_bytes=64)
+            nc.vector.quantize_mx(
+                out=t_codes[:].bitcast(FP8X4), scales=t_scales[:],
+                in_=tx1_grouped[:].rearrange("p b w j -> p (b w j)"),
+            )
+            return {"rhs": t_codes[:].bitcast(FP8X4), "rhs_scale": t_scales[:]}
+
+        def second_product(k, tx1_mx):
+            g, s = divmod(k, QUADS)
+            tx2_stage = stage2.tile([P, BPG * STEPS, PACK, C], F32)
+            h_chunk = h_grouped[:, g, s].rearrange("p b (i c) j -> p (b i) c j", c=C)
+            for j in range(PACK):
+                s2 = psum_acc.tile([P, CHUNK], F32, tag="acc")
+                nc.tensor.matmul_mx(out=s2[:], start=True, stop=True, **tx1_mx, **l_rows(j))
+                sums = s2[:].rearrange("p (q c) -> p q c", c=C)
+                if j < PACK - 1:
+                    nc.vector.scalar_tensor_tensor(
+                        out=tx2_stage[:, :, j, :], in0=sums, scalar=2.0,
+                        in1=h_chunk[:, :, :, j], op0=ALU.mult, op1=ALU.subtract,
                     )
+                else:
+                    nc.scalar.mul(out=tx2_stage[:, :, j, :], in_=sums, mul=2.0)
+                    nc.gpsimd.tensor_tensor(
+                        out=tx2_stage[:, :, j, :], in0=tx2_stage[:, :, j, :],
+                        in1=h_chunk[:, :, :, j], op=ALU.subtract,
+                    )
+            for b in range(BPG):
+                nc.sync.dma_start(
+                    out=out_1[g * BPG + b, s * STEPS : (s + 1) * STEPS].rearrange(
+                        "i (p j) c -> p i (j c)", j=PACK
+                    ),
+                    in_=tx2_stage[:, b * STEPS : (b + 1) * STEPS].rearrange(
+                        "p i j c -> p i (j c)"
+                    ),
+                )
+
+        for k in range(CHUNKS):
+            tx1_grouped = first_product(k)
+            if k + AHEAD < CHUNKS:
+                transpose_x(k + AHEAD)
+            tx1_mx = quantise_tx1(tx1_grouped)
+            if k + 1 < CHUNKS:
+                quantise_h(k + 1)
+            second_product(k, tx1_mx)

@@ -209,16 +209,16 @@ def tile_adaptivegraphconv_pa_t_kernel(tc, x, adj, out_0, out_1):
                 s2 = psum_acc.tile([P, CHUNK], F32, tag="acc")
                 nc.tensor.matmul_mx(out=s2[:], start=True, stop=True, **tx1_mx, **l_rows(j))
                 sums = s2[:].rearrange("p (q c) -> p q c", c=C)
-                if j < PACK - 1:
-                    nc.vector.scalar_tensor_tensor(
-                        out=tx2_stage[:, :, j, :], in0=sums, scalar=2.0,
-                        in1=h_chunk[:, :, :, j], op0=ALU.mult, op1=ALU.subtract,
-                    )
-                else:
+                if j == 0:
                     nc.scalar.mul(out=tx2_stage[:, :, j, :], in_=sums, mul=2.0)
                     nc.gpsimd.tensor_tensor(
                         out=tx2_stage[:, :, j, :], in0=tx2_stage[:, :, j, :],
                         in1=h_chunk[:, :, :, j], op=ALU.subtract,
+                    )
+                else:
+                    nc.vector.scalar_tensor_tensor(
+                        out=tx2_stage[:, :, j, :], in0=sums, scalar=2.0,
+                        in1=h_chunk[:, :, :, j], op0=ALU.mult, op1=ALU.subtract,
                     )
             for b in range(BPG):
                 nc.sync.dma_start(
@@ -230,11 +230,15 @@ def tile_adaptivegraphconv_pa_t_kernel(tc, x, adj, out_0, out_1):
                     ),
                 )
 
-        for k in range(CHUNKS):
-            tx1_grouped = first_product(k)
+        tx1_mx = {}
+        for k in range(CHUNKS + 1):
+            if k < CHUNKS:
+                tx1_grouped = first_product(k)
             if k + AHEAD < CHUNKS:
                 transpose_x(k + AHEAD)
-            tx1_mx = quantise_tx1(tx1_grouped)
+            if k < CHUNKS:
+                tx1_mx[k] = quantise_tx1(tx1_grouped)
             if k + 1 < CHUNKS:
                 quantise_h(k + 1)
-            second_product(k, tx1_mx)
+            if k >= 1:
+                second_product(k - 1, tx1_mx[k - 1])

@@ -36,7 +36,7 @@ def tile_adaptivegraphconv_pa_t_kernel(tc, x, adj, out_0, out_1):
         xin = ctx.enter_context(tc.tile_pool(name="xin", bufs=GROUPS))
         keep = ctx.enter_context(tc.tile_pool(name="keep", bufs=1))
         work = ctx.enter_context(tc.tile_pool(name="work", bufs=2))
-        stage1 = ctx.enter_context(tc.tile_pool(name="stage1", bufs=2 * BPG))
+        stage1 = ctx.enter_context(tc.tile_pool(name="stage1", bufs=3))
         stage2 = ctx.enter_context(tc.tile_pool(name="stage2", bufs=4))
         psum_tr = ctx.enter_context(tc.psum_pool(name="psum_tr", bufs=2))
         psum_acc = ctx.enter_context(tc.psum_pool(name="psum_acc", bufs=6))
@@ -164,6 +164,7 @@ def tile_adaptivegraphconv_pa_t_kernel(tc, x, adj, out_0, out_1):
         def first_product(k):
             g, s = divmod(k, QUADS)
             tx1_grouped = work.tile([P, BPG, P, PACK], BF16, align_bytes=64)
+            z1 = stage1.tile([P, BPG, N], F32, align_bytes=64)
             for b in range(BPG):
                 unit = {
                     "codes": h_codes[:, g, s, b, :].bitcast(FP8X4),
@@ -182,14 +183,13 @@ def tile_adaptivegraphconv_pa_t_kernel(tc, x, adj, out_0, out_1):
                     rhs=ls_codes[:].bitcast(FP8X4), rhs_scale=ls_scales[:],
                     start=True, stop=True,
                 )
-                z1 = stage1.tile([P, N], F32, align_bytes=64)
-                nc.vector.transpose(out=z1[:], in_=y1[:])
-                nc.sync.dma_start(
-                    out=out_0[g * BPG + b, s * STEPS : (s + 1) * STEPS].rearrange(
-                        "i (q v) c -> (i q) (v c)", q=SQ
-                    ),
-                    in_=z1[:],
-                )
+                nc.vector.transpose(out=z1[:, b, :], in_=y1[:])
+            nc.sync.dma_start(
+                out=out_0[g * BPG : (g + 1) * BPG, s * STEPS : (s + 1) * STEPS].rearrange(
+                    "b i (q v) c -> (i q) b (v c)", q=SQ
+                ),
+                in_=z1[:],
+            )
             return tx1_grouped
 
         def quantise_tx1(tx1_grouped):

@@ -42,7 +42,9 @@ def tile_adaptivegraphconv_pa_t_kernel(tc, x, adj, out_0, out_1):
         psum_acc = ctx.enter_context(tc.psum_pool(name="psum_acc", bufs=6))
 
         adj_rows = const.tile([P, PACK, N], BF16)
-        nc.sync.dma_start(out=adj_rows[:], in_=adj.rearrange("(p j) k -> p j k", j=PACK))
+        adj_view = adj.rearrange("(p j) k -> p j k", j=PACK)
+        nc.sync.dma_start(out=adj_rows[:, 0:2, :], in_=adj_view[:, 0:2, :])
+        nc.sync.dma_start(out=adj_rows[:, 2:4, :], in_=adj_view[:, 2:4, :])
         x_rows = x.rearrange("b c n t -> (b c) (n t)")
         x_tiles = []
         for g in range(GROUPS):
@@ -52,10 +54,12 @@ def tile_adaptivegraphconv_pa_t_kernel(tc, x, adj, out_0, out_1):
 
         ident = const.tile([P, P], F32)
         make_identity(nc, ident[:])
-        eye = const.tile([P, PACK, P, PACK], BF16)
+        eye = const.tile([P, RUN // PACK, PACK, SQ, PACK], BF16)
         nc.vector.memset(eye[:], 0.0)
         for j in range(PACK):
-            nc.vector.tensor_copy(out=eye[:, j, :, j], in_=ident[:])
+            nc.vector.tensor_copy(
+                out=eye[:, :, j, :, j], in_=ident[:].rearrange("k (q a) -> k a q", a=RUN // PACK)
+            )
         one = const.tile([P, 1], F32)
         nc.vector.memset(one[:], 1.0)
         warm = const.tile([P, 1], F32)
@@ -94,7 +98,12 @@ def tile_adaptivegraphconv_pa_t_kernel(tc, x, adj, out_0, out_1):
             )
 
         d = const.tile([P, PACK], F32)
-        nc.vector.tensor_reduce(out=d[:], in_=adj_rows[:], axis=AXIS.X, op=ALU.add)
+        nc.vector.tensor_reduce(out=d[:, 0:2], in_=adj_rows[:, 0:2, :], axis=AXIS.X, op=ALU.add)
+        unused = const.tile([P, N], BF16)
+        for j in (2, 3):
+            nc.scalar.activation(
+                out=unused[:], in_=adj_rows[:, j, :], func=ACT.Copy, accum_out=d[:, j : j + 1]
+            )
         d_safe = const.tile([P, PACK], F32)
         nc.vector.scalar_tensor_tensor(
             out=d_safe[:], in0=d[:], scalar=0.0, in1=d[:], op0=ALU.is_le, op1=ALU.add
@@ -103,56 +112,58 @@ def tile_adaptivegraphconv_pa_t_kernel(tc, x, adj, out_0, out_1):
         nc.scalar.activation(out=root[:], in_=d_safe[:], func=ACT.Sqrt)
         r_all = const.tile([P, PACK], F32)
         nc.vector.reciprocal(out=r_all[:], in_=root[:])
-        r = const.tile([P, PACK], F32)
-        nc.vector.scalar_tensor_tensor(
-            out=r[:], in0=d[:], scalar=0.0, in1=r_all[:], op0=ALU.is_gt, op1=ALU.mult
-        )
-        r_neg = const.tile([P, PACK], F32)
-        nc.vector.tensor_scalar(out=r_neg[:], in0=r[:], scalar1=-1.0, scalar2=None, op0=ALU.mult)
 
         rows_scaled = const.tile([P, PACK, PACK, P], F32)
+        r = const.tile([P, PACK], F32)
         for j in range(PACK):
             adj_by_t = adj_rows[:, j, :].rearrange("p (k t) -> p t k", t=PACK)
             if j % 2 == 0:
                 nc.vector.tensor_scalar(
-                    out=rows_scaled[:, j], in0=adj_by_t, scalar1=r_neg[:, j : j + 1],
+                    out=rows_scaled[:, j], in0=adj_by_t, scalar1=r_all[:, j : j + 1],
                     scalar2=None, op0=ALU.mult,
                 )
             else:
                 nc.scalar.activation(
-                    out=rows_scaled[:, j], in_=adj_by_t, func=ACT.Copy, scale=r_neg[:, j : j + 1]
+                    out=rows_scaled[:, j], in_=adj_by_t, func=ACT.Copy, scale=r_all[:, j : j + 1]
                 )
-        transpose_x(0)
-        l_grouped = const.tile([P, PACK, P, PACK], BF16, align_bytes=64)
+            if j == 0:
+                nc.vector.scalar_tensor_tensor(
+                    out=r[:], in0=d[:], scalar=0.0, in1=r_all[:], op0=ALU.is_gt, op1=ALU.mult
+                )
         l_spread = const.tile([P, RUN // PACK, PACK, SQ, PACK], BF16, align_bytes=64)
+        l_grouped = const.tile([P, PACK, P, PACK], BF16, align_bytes=64)
+        r_wide = r[:].unsqueeze(1).unsqueeze(1).to_broadcast([P, RUN // PACK, SQ, PACK])
         for j in range(PACK):
             lt = psum_acc.tile([P, PACK, P], F32, tag="acc")
             for t in range(PACK):
                 nc.tensor.transpose(lt[:, t, :], rows_scaled[:, j, t, :], ident[:])
-            neg_norm = work.tile([P, P, PACK], F32)
+            if j == 1:
+                transpose_x(0)
+            norm = work.tile([P, RUN // PACK, SQ, PACK], F32)
             nc.vector.tensor_tensor(
-                out=neg_norm[:], in0=lt[:].rearrange("k t p -> k p t"),
-                in1=r[:].unsqueeze(1).to_broadcast([P, P, PACK]), op=ALU.mult,
+                out=norm[:], in0=lt[:].rearrange("k t (q a) -> k a q t", a=RUN // PACK),
+                in1=r_wide, op=ALU.mult,
             )
             nc.vector.tensor_tensor(
-                out=l_grouped[:, j], in0=neg_norm[:], in1=eye[:, j], op=ALU.add
+                out=l_spread[:, :, j], in0=eye[:, :, j], in1=norm[:], op=ALU.subtract
             )
+        for j in range(PACK):
             nc.scalar.copy(
-                out=l_spread[:, :, j],
-                in_=l_grouped[:, j].rearrange("k (q a) t -> k a q t", a=RUN // PACK),
+                out=l_grouped[:, j].rearrange("k (q a) t -> k q a t", a=RUN // PACK),
+                in_=l_spread[:, :, j].rearrange("k a q t -> k q a t"),
             )
-        l_codes = const.tile([P, N], U32, align_bytes=64)
-        l_scales = const.tile([P, N], U8, align_bytes=64)
-        nc.vector.quantize_mx(
-            out=l_codes[:].bitcast(FP8X4), scales=l_scales[:],
-            in_=l_grouped[:].rearrange("k j p t -> k (j p t)"),
-        )
-        quantise_h(0)
         ls_codes = const.tile([P, N], U32, align_bytes=64)
         ls_scales = const.tile([P, N], U8, align_bytes=64)
         nc.vector.quantize_mx(
             out=ls_codes[:].bitcast(FP8X4), scales=ls_scales[:],
             in_=l_spread[:].rearrange("k a j q t -> k (a j q t)"),
+        )
+        quantise_h(0)
+        l_codes = const.tile([P, N], U32, align_bytes=64)
+        l_scales = const.tile([P, N], U8, align_bytes=64)
+        nc.vector.quantize_mx(
+            out=l_codes[:].bitcast(FP8X4), scales=l_scales[:],
+            in_=l_grouped[:].rearrange("k j p t -> k (j p t)"),
         )
         for k in range(1, AHEAD):
             transpose_x(k)
@@ -170,20 +181,30 @@ def tile_adaptivegraphconv_pa_t_kernel(tc, x, adj, out_0, out_1):
                     "codes": h_codes[:, g, s, b, :].bitcast(FP8X4),
                     "scales": h_scales[:, g, s, b, :],
                 }
-                s1 = psum_acc.tile([P, PACK, P], F32, tag="acc")
-                for j in range(PACK):
+                def spread_product():
+                    y1 = psum_acc.tile([P, N], F32, tag="acc")
                     nc.tensor.matmul_mx(
-                        out=s1[:, j, :], rhs=unit["codes"], rhs_scale=unit["scales"],
-                        start=True, stop=True, **l_rows(j),
+                        out=y1[:], lhsT=unit["codes"], lhsT_scale=unit["scales"],
+                        rhs=ls_codes[:].bitcast(FP8X4), rhs_scale=ls_scales[:],
+                        start=True, stop=True,
                     )
-                nc.scalar.copy(out=tx1_grouped[:, b], in_=s1[:].rearrange("p j w -> p w j"))
-                y1 = psum_acc.tile([P, N], F32, tag="acc")
-                nc.tensor.matmul_mx(
-                    out=y1[:], lhsT=unit["codes"], lhsT_scale=unit["scales"],
-                    rhs=ls_codes[:].bitcast(FP8X4), rhs_scale=ls_scales[:],
-                    start=True, stop=True,
-                )
-                nc.vector.transpose(out=z1[:, b, :], in_=y1[:])
+                    nc.vector.transpose(out=z1[:, b, :], in_=y1[:])
+
+                def grouped_product():
+                    s1 = psum_acc.tile([P, PACK, P], F32, tag="acc")
+                    for j in range(PACK):
+                        nc.tensor.matmul_mx(
+                            out=s1[:, j, :], rhs=unit["codes"], rhs_scale=unit["scales"],
+                            start=True, stop=True, **l_rows(j),
+                        )
+                    nc.scalar.copy(out=tx1_grouped[:, b], in_=s1[:].rearrange("p j w -> p w j"))
+
+                if b == 0:
+                    spread_product()
+                    grouped_product()
+                else:
+                    grouped_product()
+                    spread_product()
             nc.sync.dma_start(
                 out=out_0[g * BPG : (g + 1) * BPG, s * STEPS : (s + 1) * STEPS].rearrange(
                     "b i (q v) c -> (i q) b (v c)", q=SQ

@@ -24,6 +24,7 @@ CHUNKS = GROUPS * QUADS
 SQ = 32
 RUN = N // SQ
 AHEAD = 2
+LAST = BPG - 1
 
 FLOPS = 2 * 2 * N * N * B * T * C
 
@@ -176,7 +177,7 @@ def tile_adaptivegraphconv_pa_t_kernel(tc, x, adj, out_0, out_1):
             g, s = divmod(k, QUADS)
             tx1_grouped = work.tile([P, BPG, P, PACK], BF16, align_bytes=64)
             z1 = stage1.tile([P, BPG, N], F32, align_bytes=64)
-            for b in range(BPG):
+            for b in (0, LAST, 1, 2):
                 unit = {
                     "codes": h_codes[:, g, s, b, :].bitcast(FP8X4),
                     "scales": h_scales[:, g, s, b, :],
@@ -197,19 +198,40 @@ def tile_adaptivegraphconv_pa_t_kernel(tc, x, adj, out_0, out_1):
                             out=s1[:, j, :], rhs=unit["codes"], rhs_scale=unit["scales"],
                             start=True, stop=True, **l_rows(j),
                         )
-                    nc.scalar.copy(out=tx1_grouped[:, b], in_=s1[:].rearrange("p j w -> p w j"))
+                    if b != LAST:
+                        nc.scalar.copy(
+                            out=tx1_grouped[:, b], in_=s1[:].rearrange("p j w -> p w j")
+                        )
+                        return
+                    nc.scalar.copy(
+                        out=z1[:, b, :].rearrange("p (i j c) -> p j i c", j=PACK, c=C),
+                        in_=s1[:].rearrange("p j (i c) -> p j i c", c=C),
+                    )
+                    nc.gpsimd.tensor_scalar(
+                        out=tx1_grouped[:, b].rearrange("p (i c) j -> p i c j", c=C),
+                        in0=z1[:, b, :].rearrange("p (i j c) -> p i c j", j=PACK, c=C),
+                        scalar1=1.0, scalar2=0.0, op0=ALU.mult, op1=ALU.add,
+                    )
+                    nc.sync.dma_start(
+                        out=out_0[g * BPG + b, s * STEPS : (s + 1) * STEPS].rearrange(
+                            "i (p j) c -> p i (j c)", j=PACK
+                        ),
+                        in_=z1[:, b, :].rearrange("p (i w) -> p i w", i=STEPS),
+                    )
 
                 if b == 0:
                     spread_product()
+                    grouped_product()
+                elif b == LAST:
                     grouped_product()
                 else:
                     grouped_product()
                     spread_product()
             nc.sync.dma_start(
-                out=out_0[g * BPG : (g + 1) * BPG, s * STEPS : (s + 1) * STEPS].rearrange(
+                out=out_0[g * BPG : g * BPG + LAST, s * STEPS : (s + 1) * STEPS].rearrange(
                     "b i (q v) c -> (i q) b (v c)", q=SQ
                 ),
-                in_=z1[:],
+                in_=z1[:, 0:LAST, :],
             )
             return tx1_grouped
 

@@ -24,7 +24,7 @@ CHUNKS = GROUPS * QUADS
 SQ = 32
 RUN = N // SQ
 AHEAD = 2
-LAST = BPG - 1
+TWICE = 2
 
 FLOPS = 2 * 2 * N * N * B * T * C
 
@@ -177,7 +177,9 @@ def tile_adaptivegraphconv_pa_t_kernel(tc, x, adj, out_0, out_1):
             g, s = divmod(k, QUADS)
             tx1_grouped = work.tile([P, BPG, P, PACK], BF16, align_bytes=64)
             z1 = stage1.tile([P, BPG, N], F32, align_bytes=64)
-            for b in (0, LAST, 1, 2):
+            once = tuple(range(BPG - 1, TWICE - 1, -1))
+            twice = tuple(range(TWICE))
+            for b in (twice[:1] + once + twice[1:] if k == 0 else once + twice):
                 unit = {
                     "codes": h_codes[:, g, s, b, :].bitcast(FP8X4),
                     "scales": h_scales[:, g, s, b, :],
@@ -198,7 +200,7 @@ def tile_adaptivegraphconv_pa_t_kernel(tc, x, adj, out_0, out_1):
                             out=s1[:, j, :], rhs=unit["codes"], rhs_scale=unit["scales"],
                             start=True, stop=True, **l_rows(j),
                         )
-                    if b != LAST:
+                    if b < TWICE:
                         nc.scalar.copy(
                             out=tx1_grouped[:, b], in_=s1[:].rearrange("p j w -> p w j")
                         )
@@ -219,19 +221,19 @@ def tile_adaptivegraphconv_pa_t_kernel(tc, x, adj, out_0, out_1):
                         in_=z1[:, b, :].rearrange("p (i w) -> p i w", i=STEPS),
                     )
 
-                if b == 0:
-                    spread_product()
+                if b >= TWICE:
                     grouped_product()
-                elif b == LAST:
+                elif k == 0 and b == 0:
+                    spread_product()
                     grouped_product()
                 else:
                     grouped_product()
                     spread_product()
             nc.sync.dma_start(
-                out=out_0[g * BPG : g * BPG + LAST, s * STEPS : (s + 1) * STEPS].rearrange(
+                out=out_0[g * BPG : g * BPG + TWICE, s * STEPS : (s + 1) * STEPS].rearrange(
                     "b i (q v) c -> (i q) b (v c)", q=SQ
                 ),
-                in_=z1[:, 0:LAST, :],
+                in_=z1[:, 0:TWICE, :],
             )
             return tx1_grouped
 
@@ -252,17 +254,10 @@ def tile_adaptivegraphconv_pa_t_kernel(tc, x, adj, out_0, out_1):
                 s2 = psum_acc.tile([P, CHUNK], F32, tag="acc")
                 nc.tensor.matmul_mx(out=s2[:], start=True, stop=True, **tx1_mx, **l_rows(j))
                 sums = s2[:].rearrange("p (q c) -> p q c", c=C)
-                if j == 0:
-                    nc.scalar.mul(out=tx2_stage[:, :, j, :], in_=sums, mul=2.0)
-                    nc.gpsimd.tensor_tensor(
-                        out=tx2_stage[:, :, j, :], in0=tx2_stage[:, :, j, :],
-                        in1=h_chunk[:, :, :, j], op=ALU.subtract,
-                    )
-                else:
-                    nc.vector.scalar_tensor_tensor(
-                        out=tx2_stage[:, :, j, :], in0=sums, scalar=2.0,
-                        in1=h_chunk[:, :, :, j], op0=ALU.mult, op1=ALU.subtract,
-                    )
+                nc.vector.scalar_tensor_tensor(
+                    out=tx2_stage[:, :, j, :], in0=sums, scalar=2.0,
+                    in1=h_chunk[:, :, :, j], op0=ALU.mult, op1=ALU.subtract,
+                )
             for b in range(BPG):
                 nc.sync.dma_start(
                     out=out_1[g * BPG + b, s * STEPS : (s + 1) * STEPS].rearrange(

@@ -53,6 +53,10 @@ def tile_adaptivegraphconv_pa_t_kernel(tc, x, adj, out_0, out_1):
             nc.sync.dma_start(out=x_sb[:], in_=x_rows[g * P : (g + 1) * P, :])
             x_tiles.append(x_sb)
 
+        one = const.tile([P, 1], F32)
+        nc.vector.memset(one[:], 1.0)
+        warm = const.tile([P, 1], F32)
+        nc.scalar.activation(out=warm[:], in_=one[:], func=ACT.Sqrt)
         ident = const.tile([P, P], F32)
         make_identity(nc, ident[:])
         eye = const.tile([P, RUN // PACK, PACK, SQ, PACK], BF16)
@@ -61,16 +65,12 @@ def tile_adaptivegraphconv_pa_t_kernel(tc, x, adj, out_0, out_1):
             nc.vector.tensor_copy(
                 out=eye[:, :, j, :, j], in_=ident[:].rearrange("k (q a) -> k a q", a=RUN // PACK)
             )
-        one = const.tile([P, 1], F32)
-        nc.vector.memset(one[:], 1.0)
-        warm = const.tile([P, 1], F32)
-        nc.scalar.activation(out=warm[:], in_=one[:], func=ACT.Sqrt)
 
         h_grouped = keep.tile([P, GROUPS, QUADS, BPG, P, PACK], BF16, align_bytes=64)
         h_codes = keep.tile([P, GROUPS, QUADS, BPG, P], U32, align_bytes=64)
         h_scales = keep.tile([P, GROUPS, QUADS, BPG, P], U8, align_bytes=64)
 
-        def transpose_x(k):
+        def transpose_x(k, copy=nc.scalar.copy):
             g, s = divmod(k, QUADS)
             x_words = x_tiles[g][:].bitcast(F32).rearrange(
                 "r (p j u) -> r p j u", j=PACK, u=T // 2
@@ -86,9 +86,7 @@ def tile_adaptivegraphconv_pa_t_kernel(tc, x, adj, out_0, out_1):
                 )
                 for e in range(2):
                     i = 2 * half + e
-                    nc.scalar.copy(
-                        out=h_grouped[:, g, s, :, i * C : (i + 1) * C, :], in_=xt_steps[:, e]
-                    )
+                    copy(out=h_grouped[:, g, s, :, i * C : (i + 1) * C, :], in_=xt_steps[:, e])
 
         def quantise_h(k):
             g, s = divmod(k, QUADS)
@@ -226,6 +224,7 @@ def tile_adaptivegraphconv_pa_t_kernel(tc, x, adj, out_0, out_1):
                 elif k == 0 and b == 0:
                     spread_product()
                     grouped_product()
+                    quantise_h(1)
                 else:
                     grouped_product()
                     spread_product()
@@ -244,39 +243,57 @@ def tile_adaptivegraphconv_pa_t_kernel(tc, x, adj, out_0, out_1):
                 out=t_codes[:].bitcast(FP8X4), scales=t_scales[:],
                 in_=tx1_grouped[:].rearrange("p b w j -> p (b w j)"),
             )
-            return {"rhs": t_codes[:].bitcast(FP8X4), "rhs_scale": t_scales[:]}
+            return t_codes, t_scales
 
         def second_product(k, tx1_mx):
             g, s = divmod(k, QUADS)
+            t_codes, t_scales = tx1_mx
             tx2_stage = stage2.tile([P, BPG * STEPS, PACK, C], F32)
             h_chunk = h_grouped[:, g, s].rearrange("p b (i c) j -> p (b i) c j", c=C)
-            for j in range(PACK):
-                s2 = psum_acc.tile([P, CHUNK], F32, tag="acc")
-                nc.tensor.matmul_mx(out=s2[:], start=True, stop=True, **tx1_mx, **l_rows(j))
-                sums = s2[:].rearrange("p (q c) -> p q c", c=C)
-                nc.vector.scalar_tensor_tensor(
-                    out=tx2_stage[:, :, j, :], in0=sums, scalar=2.0,
-                    in1=h_chunk[:, :, :, j], op0=ALU.mult, op1=ALU.subtract,
-                )
-            for b in range(BPG):
-                nc.sync.dma_start(
-                    out=out_1[g * BPG + b, s * STEPS : (s + 1) * STEPS].rearrange(
-                        "i (p j) c -> p i (j c)", j=PACK
-                    ),
-                    in_=tx2_stage[:, b * STEPS : (b + 1) * STEPS].rearrange(
-                        "p i j c -> p i (j c)"
-                    ),
-                )
+            parts = 2 if k == CHUNKS - 1 else 1
+            width = CHUNK // parts
+            for a in range(parts):
+                cols = slice(a * width, (a + 1) * width)
+                rows = slice(a * width // C, (a + 1) * width // C)
+                for j in range(PACK):
+                    s2 = psum_acc.tile([P, CHUNK], F32, tag="acc")
+                    nc.tensor.matmul_mx(
+                        out=s2[:, 0:width], rhs=t_codes[:, cols].bitcast(FP8X4),
+                        rhs_scale=t_scales[:, cols], start=True, stop=True, **l_rows(j),
+                    )
+                    sums = s2[:, 0:width].rearrange("p (q c) -> p q c", c=C)
+                    if j == 0 and k + 1 + AHEAD >= CHUNKS:
+                        nc.scalar.mul(out=tx2_stage[:, rows, j, :], in_=sums, mul=2.0)
+                        nc.gpsimd.tensor_tensor(
+                            out=tx2_stage[:, rows, j, :], in0=tx2_stage[:, rows, j, :],
+                            in1=h_chunk[:, rows, :, j], op=ALU.subtract,
+                        )
+                    else:
+                        nc.vector.scalar_tensor_tensor(
+                            out=tx2_stage[:, rows, j, :], in0=sums, scalar=2.0,
+                            in1=h_chunk[:, rows, :, j], op0=ALU.mult, op1=ALU.subtract,
+                        )
+                for b in range(a * BPG // parts, (a + 1) * BPG // parts):
+                    nc.sync.dma_start(
+                        out=out_1[g * BPG + b, s * STEPS : (s + 1) * STEPS].rearrange(
+                            "i (p j) c -> p i (j c)", j=PACK
+                        ),
+                        in_=tx2_stage[:, b * STEPS : (b + 1) * STEPS].rearrange(
+                            "p i j c -> p i (j c)"
+                        ),
+                    )
 
         tx1_mx = {}
         for k in range(CHUNKS + 1):
             if k < CHUNKS:
                 tx1_grouped = first_product(k)
-            if k + AHEAD < CHUNKS:
+            if 0 < k < CHUNKS - AHEAD:
                 transpose_x(k + AHEAD)
             if k < CHUNKS:
                 tx1_mx[k] = quantise_tx1(tx1_grouped)
-            if k + 1 < CHUNKS:
+            if k == 0:
+                transpose_x(AHEAD, copy=nc.vector.tensor_copy)
+            if 0 < k < CHUNKS - 1:
                 quantise_h(k + 1)
             if k >= 1:
                 second_product(k - 1, tx1_mx[k - 1])

from contextlib import ExitStack

import concourse.mybir as mybir
from concourse.masks import make_identity

F32 = mybir.dt.float32
BF16 = mybir.dt.bfloat16
U32 = mybir.dt.uint32
U8 = mybir.dt.uint8
FP8X4 = mybir.dt.float8_e4m3fn_x4
ALU = mybir.AluOpType
ACT = mybir.ActivationFunctionType
AXIS = mybir.AxisListType

P = 128
PACK = 4
B, C, N, T = 16, 32, 512, 12
BPG = P // C
GROUPS = B // BPG
STEPS = P // C
QUADS = T // STEPS
CHUNK = BPG * P
CHUNKS = GROUPS * QUADS
SQ = 32
RUN = N // SQ
AHEAD = 2
TWICE = 2

FLOPS = 2 * 2 * N * N * B * T * C


def tile_adaptivegraphconv_pa_t_kernel(tc, x, adj, out_0, out_1):
    nc = tc.nc
    with ExitStack() as ctx:
        ctx.enter_context(tc.manual_schedule())
        const = ctx.enter_context(tc.tile_pool(name="const", bufs=1))
        xin = ctx.enter_context(tc.tile_pool(name="xin", bufs=GROUPS))
        keep = ctx.enter_context(tc.tile_pool(name="keep", bufs=1))
        work = ctx.enter_context(tc.tile_pool(name="work", bufs=2))
        stage1 = ctx.enter_context(tc.tile_pool(name="stage1", bufs=3))
        stage2 = ctx.enter_context(tc.tile_pool(name="stage2", bufs=4))
        psum_tr = ctx.enter_context(tc.psum_pool(name="psum_tr", bufs=2))
        psum_acc = ctx.enter_context(tc.psum_pool(name="psum_acc", bufs=6))

        adj_rows = const.tile([P, PACK, N], BF16)
        adj_view = adj.rearrange("(p j) k -> p j k", j=PACK)
        nc.sync.dma_start(out=adj_rows[:, 0:2, :], in_=adj_view[:, 0:2, :])
        nc.sync.dma_start(out=adj_rows[:, 2:4, :], in_=adj_view[:, 2:4, :])
        x_rows = x.rearrange("b c n t -> (b c) (n t)")
        x_tiles = []
        for g in range(GROUPS):
            x_sb = xin.tile([P, N * T], BF16, name="x_sb")
            nc.sync.dma_start(out=x_sb[:], in_=x_rows[g * P : (g + 1) * P, :])
            x_tiles.append(x_sb)

        one = const.tile([P, 1], F32)
        nc.vector.memset(one[:], 1.0)
        warm = const.tile([P, 1], F32)
        nc.scalar.activation(out=warm[:], in_=one[:], func=ACT.Sqrt)
        ident = const.tile([P, P], F32)
        make_identity(nc, ident[:])
        eye = const.tile([P, RUN // PACK, PACK, SQ, PACK], BF16)
        nc.vector.memset(eye[:], 0.0)
        for j in range(PACK):
            nc.vector.tensor_copy(
                out=eye[:, :, j, :, j], in_=ident[:].rearrange("k (q a) -> k a q", a=RUN // PACK)
            )

        h_grouped = keep.tile([P, GROUPS, QUADS, BPG, P, PACK], BF16, align_bytes=64)
        h_codes = keep.tile([P, GROUPS, QUADS, BPG, P], U32, align_bytes=64)
        h_scales = keep.tile([P, GROUPS, QUADS, BPG, P], U8, align_bytes=64)

        def transpose_x(k, copy=nc.scalar.copy):
            g, s = divmod(k, QUADS)
            x_words = x_tiles[g][:].bitcast(F32).rearrange(
                "r (p j u) -> r p j u", j=PACK, u=T // 2
            )
            for half in range(STEPS // 2):
                xt = psum_tr.tile([P, PACK, P], F32)
                for j in range(PACK):
                    nc.tensor.transpose(
                        xt[:, j, :], x_words[:, :, j, s * (STEPS // 2) + half], ident[:]
                    )
                xt_steps = xt[:].rearrange("p j w -> p (j w)").bitcast(BF16).rearrange(
                    "p (j b c e) -> p e b c j", j=PACK, b=BPG, e=2
                )
                for e in range(2):
                    i = 2 * half + e
                    copy(out=h_grouped[:, g, s, :, i * C : (i + 1) * C, :], in_=xt_steps[:, e])

        def quantise_h(k):
            g, s = divmod(k, QUADS)
            nc.vector.quantize_mx(
                out=h_codes[:, g, s].rearrange("p b w -> p (b w)").bitcast(FP8X4),
                scales=h_scales[:, g, s].rearrange("p b w -> p (b w)"),
                in_=h_grouped[:, g, s].rearrange("p b w j -> p (b w j)"),
            )

        d = const.tile([P, PACK], F32)
        nc.vector.tensor_reduce(out=d[:, 0:2], in_=adj_rows[:, 0:2, :], axis=AXIS.X, op=ALU.add)
        unused = const.tile([P, N], BF16)
        for j in (2, 3):
            nc.scalar.activation(
                out=unused[:], in_=adj_rows[:, j, :], func=ACT.Copy, accum_out=d[:, j : j + 1]
            )
        d_safe = const.tile([P, PACK], F32)
        nc.vector.scalar_tensor_tensor(
            out=d_safe[:], in0=d[:], scalar=0.0, in1=d[:], op0=ALU.is_le, op1=ALU.add
        )
        root = const.tile([P, PACK], F32)
        nc.scalar.activation(out=root[:], in_=d_safe[:], func=ACT.Sqrt)
        r_all = const.tile([P, PACK], F32)
        nc.vector.reciprocal(out=r_all[:], in_=root[:])

        rows_scaled = const.tile([P, PACK, PACK, P], F32)
        r = const.tile([P, PACK], F32)
        for j in range(PACK):
            adj_by_t = adj_rows[:, j, :].rearrange("p (k t) -> p t k", t=PACK)
            if j % 2 == 0:
                nc.vector.tensor_scalar(
                    out=rows_scaled[:, j], in0=adj_by_t, scalar1=r_all[:, j : j + 1],
                    scalar2=None, op0=ALU.mult,
                )
            else:
                nc.scalar.activation(
                    out=rows_scaled[:, j], in_=adj_by_t, func=ACT.Copy, scale=r_all[:, j : j + 1]
                )
            if j == 0:
                nc.vector.scalar_tensor_tensor(
                    out=r[:], in0=d[:], scalar=0.0, in1=r_all[:], op0=ALU.is_gt, op1=ALU.mult
                )
        l_spread = const.tile([P, RUN // PACK, PACK, SQ, PACK], BF16, align_bytes=64)
        l_grouped = const.tile([P, PACK, P, PACK], BF16, align_bytes=64)
        r_wide = r[:].unsqueeze(1).unsqueeze(1).to_broadcast([P, RUN // PACK, SQ, PACK])
        for j in range(PACK):
            lt = psum_acc.tile([P, PACK, P], F32, tag="acc")
            for t in range(PACK):
                nc.tensor.transpose(lt[:, t, :], rows_scaled[:, j, t, :], ident[:])
            if j == 1:
                transpose_x(0)
            norm = work.tile([P, RUN // PACK, SQ, PACK], F32)
            nc.vector.tensor_tensor(
                out=norm[:], in0=lt[:].rearrange("k t (q a) -> k a q t", a=RUN // PACK),
                in1=r_wide, op=ALU.mult,
            )
            nc.vector.tensor_tensor(
                out=l_spread[:, :, j], in0=eye[:, :, j], in1=norm[:], op=ALU.subtract
            )
        for j in range(PACK):
            nc.scalar.copy(
                out=l_grouped[:, j].rearrange("k (q a) t -> k q a t", a=RUN // PACK),
                in_=l_spread[:, :, j].rearrange("k a q t -> k q a t"),
            )
        ls_codes = const.tile([P, N], U32, align_bytes=64)
        ls_scales = const.tile([P, N], U8, align_bytes=64)
        nc.vector.quantize_mx(
            out=ls_codes[:].bitcast(FP8X4), scales=ls_scales[:],
            in_=l_spread[:].rearrange("k a j q t -> k (a j q t)"),
        )
        quantise_h(0)
        l_codes = const.tile([P, N], U32, align_bytes=64)
        l_scales = const.tile([P, N], U8, align_bytes=64)
        nc.vector.quantize_mx(
            out=l_codes[:].bitcast(FP8X4), scales=l_scales[:],
            in_=l_grouped[:].rearrange("k j p t -> k (j p t)"),
        )
        for k in range(1, AHEAD):
            transpose_x(k)

        def l_rows(j):
            cols = slice(j * P, (j + 1) * P)
            return {"lhsT": l_codes[:, cols].bitcast(FP8X4), "lhsT_scale": l_scales[:, cols]}

        def first_product(k):
            g, s = divmod(k, QUADS)
            tx1_grouped = work.tile([P, BPG, P, PACK], BF16, align_bytes=64)
            z1 = stage1.tile([P, BPG, N], F32, align_bytes=64)
            once = tuple(range(BPG - 1, TWICE - 1, -1))
            twice = tuple(range(TWICE))
            for b in (twice[:1] + once + twice[1:] if k == 0 else once + twice):
                unit = {
                    "codes": h_codes[:, g, s, b, :].bitcast(FP8X4),
                    "scales": h_scales[:, g, s, b, :],
                }
                def spread_product():
                    y1 = psum_acc.tile([P, N], F32, tag="acc")
                    nc.tensor.matmul_mx(
                        out=y1[:], lhsT=unit["codes"], lhsT_scale=unit["scales"],
                        rhs=ls_codes[:].bitcast(FP8X4), rhs_scale=ls_scales[:],
                        start=True, stop=True,
                    )
                    nc.vector.transpose(out=z1[:, b, :], in_=y1[:])

                def grouped_product():
                    s1 = psum_acc.tile([P, PACK, P], F32, tag="acc")
                    for j in range(PACK):
                        nc.tensor.matmul_mx(
                            out=s1[:, j, :], rhs=unit["codes"], rhs_scale=unit["scales"],
                            start=True, stop=True, **l_rows(j),
                        )
                    if b < TWICE:
                        nc.scalar.copy(
                            out=tx1_grouped[:, b], in_=s1[:].rearrange("p j w -> p w j")
                        )
                        return
                    nc.scalar.copy(
                        out=z1[:, b, :].rearrange("p (i j c) -> p j i c", j=PACK, c=C),
                        in_=s1[:].rearrange("p j (i c) -> p j i c", c=C),
                    )
                    nc.gpsimd.tensor_scalar(
                        out=tx1_grouped[:, b].rearrange("p (i c) j -> p i c j", c=C),
                        in0=z1[:, b, :].rearrange("p (i j c) -> p i c j", j=PACK, c=C),
                        scalar1=1.0, scalar2=0.0, op0=ALU.mult, op1=ALU.add,
                    )
                    nc.sync.dma_start(
                        out=out_0[g * BPG + b, s * STEPS : (s + 1) * STEPS].rearrange(
                            "i (p j) c -> p i (j c)", j=PACK
                        ),
                        in_=z1[:, b, :].rearrange("p (i w) -> p i w", i=STEPS),
                    )

                if b >= TWICE:
                    grouped_product()
                elif k == 0 and b == 0:
                    spread_product()
                    grouped_product()
                    quantise_h(1)
                else:
                    grouped_product()
                    spread_product()
            nc.sync.dma_start(
                out=out_0[g * BPG : g * BPG + TWICE, s * STEPS : (s + 1) * STEPS].rearrange(
                    "b i (q v) c -> (i q) b (v c)", q=SQ
                ),
                in_=z1[:, 0:TWICE, :],
            )
            return tx1_grouped

        def quantise_tx1(tx1_grouped):
            t_codes = work.tile([P, CHUNK], U32, align_bytes=64)
            t_scales = work.tile([P, CHUNK], U8, align_bytes=64)
            nc.vector.quantize_mx(
                out=t_codes[:].bitcast(FP8X4), scales=t_scales[:],
                in_=tx1_grouped[:].rearrange("p b w j -> p (b w j)"),
            )
            return t_codes, t_scales

        def second_product(k, tx1_mx):
            g, s = divmod(k, QUADS)
            t_codes, t_scales = tx1_mx
            tx2_stage = stage2.tile([P, BPG * STEPS, PACK, C], F32)
            h_chunk = h_grouped[:, g, s].rearrange("p b (i c) j -> p (b i) c j", c=C)
            parts = 2 if k == CHUNKS - 1 else 1
            width = CHUNK // parts
            for a in range(parts):
                cols = slice(a * width, (a + 1) * width)
                rows = slice(a * width // C, (a + 1) * width // C)
                for j in range(PACK):
                    s2 = psum_acc.tile([P, CHUNK], F32, tag="acc")
                    nc.tensor.matmul_mx(
                        out=s2[:, 0:width], rhs=t_codes[:, cols].bitcast(FP8X4),
                        rhs_scale=t_scales[:, cols], start=True, stop=True, **l_rows(j),
                    )
                    sums = s2[:, 0:width].rearrange("p (q c) -> p q c", c=C)
                    if j == 0 and k + 1 + AHEAD >= CHUNKS:
                        nc.scalar.mul(out=tx2_stage[:, rows, j, :], in_=sums, mul=2.0)
                        nc.gpsimd.tensor_tensor(
                            out=tx2_stage[:, rows, j, :], in0=tx2_stage[:, rows, j, :],
                            in1=h_chunk[:, rows, :, j], op=ALU.subtract,
                        )
                    else:
                        nc.vector.scalar_tensor_tensor(
                            out=tx2_stage[:, rows, j, :], in0=sums, scalar=2.0,
                            in1=h_chunk[:, rows, :, j], op0=ALU.mult, op1=ALU.subtract,
                        )
                for b in range(a * BPG // parts, (a + 1) * BPG // parts):
                    nc.sync.dma_start(
                        out=out_1[g * BPG + b, s * STEPS : (s + 1) * STEPS].rearrange(
                            "i (p j) c -> p i (j c)", j=PACK
                        ),
                        in_=tx2_stage[:, b * STEPS : (b + 1) * STEPS].rearrange(
                            "p i j c -> p i (j c)"
                        ),
                    )

        tx1_mx = {}
        for k in range(CHUNKS + 1):
            if k < CHUNKS:
                tx1_grouped = first_product(k)
            if 0 < k < CHUNKS - AHEAD:
                transpose_x(k + AHEAD)
            if k < CHUNKS:
                tx1_mx[k] = quantise_tx1(tx1_grouped)
            if k == 0:
                transpose_x(AHEAD, copy=nc.vector.tensor_copy)
            if 0 < k < CHUNKS - 1:
                quantise_h(k + 1)
            if k >= 1:
                second_product(k - 1, tx1_mx[k - 1])
